import numpy as np
import ml_dtypes

BF16 = ml_dtypes.bfloat16


def bf(x):
    return np.asarray(x, np.float32).astype(BF16)


def f32(x):
    return np.asarray(x, np.float32)


def f64(x):
    return np.asarray(x).astype(np.float64)


def striped(idx):
    return np.tile(idx.reshape(-1, 16).T, (8, 1))


F, S, T, TN, M, R, H, N = 128, 1024, 16, 8, 128, 8, 512, 4096


def setup_inputs():
    return {"table": bf(np.random.standard_normal((F, S))), "templates": bf(np.random.uniform(size=(F, M))), "offs": striped(np.concatenate([np.random.permutation(S)[:H] for _ in range(R)]))}


def reference(table, templates, offs):
    idx = offs[:16].T.reshape(-1)
    xg = f64(table)[:, idx]
    w = f64(templates)
    return (np.sum(xg * xg, axis=0)[None, :] + np.sum(w * w, axis=0)[:, None] - 2.0 * (w.T @ xg)) / F

@@ -1,0 +1,60 @@
+import concourse.mybir as mybir
+
+BF16, F32, U16 = mybir.dt.bfloat16, mybir.dt.float32, mybir.dt.uint16
+MULT, ADD = mybir.AluOpType.mult, mybir.AluOpType.add
+IDENTITY = mybir.ActivationFunctionType.Identity
+
+F = 128
+S = 1024
+M = 128
+N = 4096
+PIECE = 512
+N_PIECES = N // PIECE
+PIECE_COLS = PIECE // 16
+
+FLOPS = 2 * F * M * N + 2 * F * N + 2 * F * M + 3 * M * N
+
+
+def tile_ot_gnn_layer_kernel(tc, table, templates, offs, out):
+    nc = tc.nc
+    with (
+        tc.tile_pool(name="held", bufs=1) as held,
+        tc.tile_pool(name="staging", bufs=N_PIECES) as staging,
+        tc.psum_pool(name="norm_bank", bufs=1) as norm_bank,
+        tc.psum_pool(name="banks", bufs=4) as banks,
+    ):
+        temps = held.tile([F, M], BF16, name="temps")
+        nc.sync.dma_start(temps[:], templates)
+        offsets = held.tile([128, N // 16], U16, name="offsets")
+        nc.sync.dma_start(offsets[:], offs)
+        nodes = held.tile([F, S], BF16, name="nodes")
+        nc.scalar.dma_start(nodes[:], table)
+
+        minus_half = held.tile([F, M], BF16, name="minus_half")
+        nc.vector.memset(minus_half[:], -0.5)
+        one_over_f = held.tile([F, 1], BF16, name="one_over_f")
+        nc.vector.memset(one_over_f[:], 1.0 / F)
+
+        temps_sq = held.tile([F, M], BF16, name="temps_sq")
+        nc.vector.tensor_tensor(temps_sq[:], temps[:], temps[:], MULT)
+        temp_norm_psum = norm_bank.tile([M, 1], F32, name="temp_norm_psum")
+        nc.tensor.matmul(temp_norm_psum[:], temps_sq[:], one_over_f[:], start=True, stop=True)
+
+        nodes_sq = held.tile([F, S], BF16, name="nodes_sq")
+        nc.vector.tensor_tensor(nodes_sq[:], nodes[:], nodes[:], MULT)
+
+        temp_norm = held.tile([M, 1], F32, name="temp_norm")
+        nc.vector.tensor_copy(temp_norm[:], temp_norm_psum[:])
+
+        for k in range(N_PIECES):
+            piece = offsets[:, k * PIECE_COLS : (k + 1) * PIECE_COLS]
+            bank = banks.tile([M, PIECE], F32, name="bank")
+            nc.tensor.matmul(bank[:], temps[:], nodes[:].indirect(piece), start=True, stop=False)
+            nc.tensor.matmul(bank[:], minus_half[:], nodes_sq[:].indirect(piece), start=False, stop=True)
+
+            cost = staging.tile([M, PIECE], F32, name="cost")
+            if k % 2 == 0:
+                nc.vector.tensor_scalar(cost[:], bank[:], -2.0 / F, temp_norm[:], MULT, ADD)
+            else:
+                nc.scalar.activation(cost[:], bank[:], IDENTITY, bias=temp_norm[:], scale=-2.0 / F)
+            nc.sync.dma_start(out[:, k * PIECE : (k + 1) * PIECE], cost[:])

@@ -10,6 +10,7 @@ M = 128
 N = 4096
 PIECE = 512
 N_PIECES = N // PIECE
+N_WARM = 4
 PIECE_COLS = PIECE // 16
 
 FLOPS = 2 * F * M * N + 2 * F * N + 2 * F * M + 3 * M * N
@@ -21,6 +22,7 @@ def tile_ot_gnn_layer_kernel(tc, table, templates, offs, out):
         tc.tile_pool(name="held", bufs=1) as held,
         tc.tile_pool(name="staging", bufs=N_PIECES) as staging,
         tc.psum_pool(name="norm_bank", bufs=1) as norm_bank,
+        tc.psum_pool(name="warm_bank", bufs=1) as warm_bank,
         tc.psum_pool(name="banks", bufs=4) as banks,
     ):
         temps = held.tile([F, M], BF16, name="temps")
@@ -34,6 +36,12 @@ def tile_ot_gnn_layer_kernel(tc, table, templates, offs, out):
         nc.vector.memset(minus_half[:], -0.5)
         one_over_f = held.tile([F, 1], BF16, name="one_over_f")
         nc.vector.memset(one_over_f[:], 1.0 / F)
+
+        warm_moving = held.tile([F, PIECE], BF16, name="warm_moving")
+        nc.vector.memset(warm_moving[:], 0.0)
+        warm_product = warm_bank.tile([M, PIECE], F32, name="warm_product")
+        for w in range(N_WARM):
+            nc.tensor.matmul(warm_product[:], minus_half[:], warm_moving[:], start=True, stop=True)
 
         temps_sq = held.tile([F, M], BF16, name="temps_sq")
         nc.vector.tensor_tensor(temps_sq[:], temps[:], temps[:], MULT)

@@ -10,8 +10,8 @@ M = 128
 N = 4096
 PIECE = 512
 N_PIECES = N // PIECE
-N_WARM = 4
 PIECE_COLS = PIECE // 16
+HALF = PIECE // 2
 
 FLOPS = 2 * F * M * N + 2 * F * N + 2 * F * M + 3 * M * N
 
@@ -22,7 +22,6 @@ def tile_ot_gnn_layer_kernel(tc, table, templates, offs, out):
         tc.tile_pool(name="held", bufs=1) as held,
         tc.tile_pool(name="staging", bufs=N_PIECES) as staging,
         tc.psum_pool(name="norm_bank", bufs=1) as norm_bank,
-        tc.psum_pool(name="warm_bank", bufs=1) as warm_bank,
         tc.psum_pool(name="banks", bufs=4) as banks,
     ):
         temps = held.tile([F, M], BF16, name="temps")
@@ -36,12 +35,6 @@ def tile_ot_gnn_layer_kernel(tc, table, templates, offs, out):
         nc.vector.memset(minus_half[:], -0.5)
         one_over_f = held.tile([F, 1], BF16, name="one_over_f")
         nc.vector.memset(one_over_f[:], 1.0 / F)
-
-        warm_moving = held.tile([F, PIECE], BF16, name="warm_moving")
-        nc.vector.memset(warm_moving[:], 0.0)
-        warm_product = warm_bank.tile([M, PIECE], F32, name="warm_product")
-        for w in range(N_WARM):
-            nc.tensor.matmul(warm_product[:], minus_half[:], warm_moving[:], start=True, stop=True)
 
         temps_sq = held.tile([F, M], BF16, name="temps_sq")
         nc.vector.tensor_tensor(temps_sq[:], temps[:], temps[:], MULT)
@@ -61,8 +54,11 @@ def tile_ot_gnn_layer_kernel(tc, table, templates, offs, out):
             nc.tensor.matmul(bank[:], minus_half[:], nodes_sq[:].indirect(piece), start=False, stop=True)
 
             cost = staging.tile([M, PIECE], F32, name="cost")
-            if k % 2 == 0:
-                nc.vector.tensor_scalar(cost[:], bank[:], -2.0 / F, temp_norm[:], MULT, ADD)
-            else:
-                nc.scalar.activation(cost[:], bank[:], IDENTITY, bias=temp_norm[:], scale=-2.0 / F)
-            nc.sync.dma_start(out[:, k * PIECE : (k + 1) * PIECE], cost[:])
+            for h in range(2):
+                cols = slice(h * HALF, (h + 1) * HALF)
+                if k % 2 == 0:
+                    nc.scalar.activation(cost[:, cols], bank[:, cols], IDENTITY, bias=temp_norm[:], scale=-2.0 / F)
+                else:
+                    nc.vector.tensor_scalar(cost[:, cols], bank[:, cols], -2.0 / F, temp_norm[:], MULT, ADD)
+                first = k * PIECE + h * HALF
+                nc.sync.dma_start(out[:, first : first + HALF], cost[:, cols])

@@ -11,6 +11,7 @@ N = 4096
 PIECE = 512
 N_PIECES = N // PIECE
 PIECE_COLS = PIECE // 16
+TABLE_LOADS = 4
 HALF = PIECE // 2
 
 FLOPS = 2 * F * M * N + 2 * F * N + 2 * F * M + 3 * M * N
@@ -29,7 +30,10 @@ def tile_ot_gnn_layer_kernel(tc, table, templates, offs, out):
         offsets = held.tile([128, N // 16], U16, name="offsets")
         nc.sync.dma_start(offsets[:], offs)
         nodes = held.tile([F, S], BF16, name="nodes")
-        nc.scalar.dma_start(nodes[:], table)
+        for b in range(TABLE_LOADS):
+            cols = slice(b * (S // TABLE_LOADS), (b + 1) * (S // TABLE_LOADS))
+            queue = nc.scalar if b % 2 == 0 else nc.sync
+            queue.dma_start(nodes[:, cols], table[:, cols])
 
         minus_half = held.tile([F, M], BF16, name="minus_half")
         nc.vector.memset(minus_half[:], -0.5)

@@ -1,4 +1,5 @@
 import concourse.mybir as mybir
+from concourse.masks import make_identity
 
 BF16, F32, U16 = mybir.dt.bfloat16, mybir.dt.float32, mybir.dt.uint16
 MULT, ADD = mybir.AluOpType.mult, mybir.AluOpType.add
@@ -37,19 +38,18 @@ def tile_ot_gnn_layer_kernel(tc, table, templates, offs, out):
 
         minus_half = held.tile([F, M], BF16, name="minus_half")
         nc.vector.memset(minus_half[:], -0.5)
-        one_over_f = held.tile([F, 1], BF16, name="one_over_f")
-        nc.vector.memset(one_over_f[:], 1.0 / F)
+        identity = held.tile([M, M], F32, name="identity")
+        make_identity(nc, identity[:])
 
-        temps_sq = held.tile([F, M], BF16, name="temps_sq")
-        nc.vector.tensor_tensor(temps_sq[:], temps[:], temps[:], MULT)
-        temp_norm_psum = norm_bank.tile([M, 1], F32, name="temp_norm_psum")
-        nc.tensor.matmul(temp_norm_psum[:], temps_sq[:], one_over_f[:], start=True, stop=True)
+        gram = norm_bank.tile([M, M], F32, name="gram")
+        nc.tensor.matmul(gram[:], temps[:], temps[:], start=True, stop=True)
 
         nodes_sq = held.tile([F, S], BF16, name="nodes_sq")
         nc.vector.tensor_tensor(nodes_sq[:], nodes[:], nodes[:], MULT)
 
+        diagonal = held.tile([M, M], F32, name="diagonal")
         temp_norm = held.tile([M, 1], F32, name="temp_norm")
-        nc.vector.tensor_copy(temp_norm[:], temp_norm_psum[:])
+        nc.vector.scalar_tensor_tensor(diagonal[:], gram[:], 1.0 / F, identity[:], MULT, MULT, accum_out=temp_norm[:])
 
         for k in range(N_PIECES):
             piece = offsets[:, k * PIECE_COLS : (k + 1) * PIECE_COLS]

import concourse.mybir as mybir
from concourse.masks import make_identity

BF16, F32, U16 = mybir.dt.bfloat16, mybir.dt.float32, mybir.dt.uint16
MULT, ADD = mybir.AluOpType.mult, mybir.AluOpType.add
IDENTITY = mybir.ActivationFunctionType.Identity

F = 128
S = 1024
M = 128
N = 4096
PIECE = 512
N_PIECES = N // PIECE
PIECE_COLS = PIECE // 16
TABLE_LOADS = 4
HALF = PIECE // 2

FLOPS = 2 * F * M * N + 2 * F * N + 2 * F * M + 3 * M * N


def tile_ot_gnn_layer_kernel(tc, table, templates, offs, out):
    nc = tc.nc
    with (
        tc.tile_pool(name="held", bufs=1) as held,
        tc.tile_pool(name="staging", bufs=N_PIECES) as staging,
        tc.psum_pool(name="norm_bank", bufs=1) as norm_bank,
        tc.psum_pool(name="banks", bufs=4) as banks,
    ):
        temps = held.tile([F, M], BF16, name="temps")
        nc.sync.dma_start(temps[:], templates)
        offsets = held.tile([128, N // 16], U16, name="offsets")
        nc.sync.dma_start(offsets[:], offs)
        nodes = held.tile([F, S], BF16, name="nodes")
        for b in range(TABLE_LOADS):
            cols = slice(b * (S // TABLE_LOADS), (b + 1) * (S // TABLE_LOADS))
            queue = nc.scalar if b % 2 == 0 else nc.sync
            queue.dma_start(nodes[:, cols], table[:, cols])

        minus_half = held.tile([F, M], BF16, name="minus_half")
        nc.vector.memset(minus_half[:], -0.5)
        identity = held.tile([M, M], F32, name="identity")
        make_identity(nc, identity[:])

        gram = norm_bank.tile([M, M], F32, name="gram")
        nc.tensor.matmul(gram[:], temps[:], temps[:], start=True, stop=True)

        nodes_sq = held.tile([F, S], BF16, name="nodes_sq")
        nc.vector.tensor_tensor(nodes_sq[:], nodes[:], nodes[:], MULT)

        diagonal = held.tile([M, M], F32, name="diagonal")
        temp_norm = held.tile([M, 1], F32, name="temp_norm")
        nc.vector.scalar_tensor_tensor(diagonal[:], gram[:], 1.0 / F, identity[:], MULT, MULT, accum_out=temp_norm[:])

        for k in range(N_PIECES):
            piece = offsets[:, k * PIECE_COLS : (k + 1) * PIECE_COLS]
            bank = banks.tile([M, PIECE], F32, name="bank")
            nc.tensor.matmul(bank[:], temps[:], nodes[:].indirect(piece), start=True, stop=False)
            nc.tensor.matmul(bank[:], minus_half[:], nodes_sq[:].indirect(piece), start=False, stop=True)

            cost = staging.tile([M, PIECE], F32, name="cost")
            for h in range(2):
                cols = slice(h * HALF, (h + 1) * HALF)
                if k % 2 == 0:
                    nc.scalar.activation(cost[:, cols], bank[:, cols], IDENTITY, bias=temp_norm[:], scale=-2.0 / F)
                else:
                    nc.vector.tensor_scalar(cost[:, cols], bank[:, cols], -2.0 / F, temp_norm[:], MULT, ADD)
                first = k * PIECE + h * HALF
                nc.sync.dma_start(out[:, first : first + HALF], cost[:, cols])
